import numpy as np
import ml_dtypes


def mxq(x, axis, fmt="e4m3"):
    dtype, down = {"e4m3": (ml_dtypes.float8_e4m3fn, 7), "e5m2": (ml_dtypes.float8_e5m2, 14)}[fmt]
    v = np.moveaxis(np.asarray(x, np.float32).astype(ml_dtypes.bfloat16).astype(np.float64), axis, -1)
    blocks = v.reshape(v.shape[:-1] + (-1, 32))
    amax = np.abs(blocks).max(-1, keepdims=True)
    byte = np.maximum(np.where(amax > 0, np.frexp(amax)[1] - 1 + 127, 0) - down, 1)
    scale = np.exp2(byte - 127.0)
    codes = (blocks / scale).astype(np.float32).astype(dtype).astype(np.float64)
    return np.moveaxis((codes * scale).reshape(v.shape), -1, axis)


WIDE = False


def mx_kscale(k):
    if not WIDE:
        return np.ones(k)
    levels = np.array([18, -18])
    if k % 512:
        return np.exp2(np.random.permutation(np.resize(levels, k // 32))).repeat(32)
    a = np.empty((k // 512, 16))
    for p in range(k // 512):
        a[p, :8] = np.random.permutation(np.resize(levels, 8))
        for g in range(8):
            far = levels[np.abs(levels - a[p, g]) >= 10]
            a[p, g + 8] = far[np.random.randint(len(far))]
    return np.exp2(a.ravel()).repeat(32)


BF16 = ml_dtypes.bfloat16


def bf(x):
    return np.asarray(x, np.float32).astype(BF16)


def f64(x):
    return np.asarray(x).astype(np.float64)


N, B, T = 1024, 4, 512


def inv_sqrt_degree(W):
    deg = W.sum(axis=0)
    return np.where(deg > 0, np.where(deg > 0, deg, 1.0) ** -0.5, 0.0)


def setup_inputs():
    s = mx_kscale(N)
    u = mx_kscale(N)
    v = mx_kscale(T)
    p = np.random.random(N)
    p = np.where(p < 0.05, 0.0, p)
    edge = np.random.random((N, N)) < p[None, :]
    x0 = bf(np.random.standard_normal((B, T, N)) * 2.0)
    e0 = bf(edge * 0.4 * N * (0.5 + np.random.random((N, N))))
    w0 = bf(np.random.standard_normal((T, T)) * 3.0 / np.sqrt(T))
    bias = bf(np.random.standard_normal(T) * 0.1)
    g = bf(np.random.standard_normal((B, T, N)) * np.exp2(np.random.randint(-6, 1, (B, T, 1))) * 8.0 * u[None, None, :] * v[None, :, None])
    dinv = inv_sqrt_degree(f64(e0))
    return {"x": bf(f64(x0) * s[None, None, :]),
            "edge_w": bf(f64(e0) / s[:, None] / u[None, :]),
            "weight": bf(f64(w0) / v[None, :]),
            "bias": bias,
            "dinv": np.asarray(dinv, np.float32),
            "grad_out": g}


def reference(x, edge_w, weight, bias, dinv, grad_out):
    dv = f64(dinv)
    dz2 = (f64(grad_out) * dv[None, None, :]).reshape(B * T, N)
    dh = mxq(dz2, 1, "e5m2") @ mxq(f64(edge_w), 1, "e4m3").T
    dz1 = dh.reshape(B, T, N) * dv[None, None, :]
    z = dz1.transpose(0, 2, 1).reshape(B * N, T)
    xt = f64(x).transpose(0, 2, 1).reshape(B * N, T)
    dx = mxq(z, 1, "e5m2") @ mxq(f64(weight), 1, "e4m3").T
    dweight = mxq(xt, 0, "e4m3").T @ mxq(z, 0, "e5m2")
    return dx.reshape(B, N, T).transpose(0, 2, 1), dweight

@@ -1,0 +1,292 @@
+from contextlib import ExitStack
+
+import concourse.mybir as mybir
+from concourse.masks import make_identity
+
+B, T, O, N = 4, 512, 512, 1024
+FLOPS = 2 * B * O * N * N + 2 * 2 * B * N * O * T
+
+F32 = mybir.dt.float32
+BF16 = mybir.dt.bfloat16
+U32 = mybir.dt.uint32
+U8 = mybir.dt.uint8
+E4M3 = mybir.dt.float8_e4m3fn_x4
+E5M2 = mybir.dt.float8_e5m2_x4
+ACT = mybir.ActivationFunctionType
+ALU = mybir.AluOpType
+
+P = 128
+HALVES = 2 * B
+GROUPED_BUFS = {"gt": 3, "zt": 3, "xt": 2, "f": 2}
+
+
+def tile_graphembedding_pa_v_kernel(tc, x, edge_w, weight, bias, dinv, grad_out, out_0, out_1):
+    nc = tc.nc
+    with ExitStack() as ctx:
+        const = ctx.enter_context(tc.tile_pool(name="const", bufs=1))
+        loads = ctx.enter_context(tc.tile_pool(name="loads", bufs=1))
+        keep = ctx.enter_context(tc.tile_pool(name="keep", bufs=1))
+        work = ctx.enter_context(tc.tile_pool(name="work", bufs=3))
+        psum = ctx.enter_context(tc.psum_pool(name="psum", bufs=8))
+
+        ident = const.tile([P, P], F32, name="ident")
+        make_identity(nc, ident[:])
+        dv = const.tile([P, 2, 4], F32, name="dv")
+
+        ctx.enter_context(tc.manual_schedule())
+
+        g_sb = [loads.tile([P, 4, N], BF16, name=f"g{b}") for b in range(B)]
+        x_sb = [loads.tile([P, 4, N], BF16, name=f"x{b}") for b in range(B)]
+        e_sb = [loads.tile([P, 4, N], BF16, name=f"e{j}") for j in range(2)]
+        w_sb = loads.tile([P, 4, O], BF16, name="w_sb")
+
+        def load_rows(tile, src, lo, hi):
+            view = src.rearrange("(p j) k -> p j k", j=4)
+            nc.sync.dma_start(out=tile[:, lo:hi, :], in_=view[:, lo:hi, :])
+
+        load_rows(g_sb[0], grad_out[0], 0, 2)
+        nc.sync.dma_start(out=dv[:], in_=dinv.rearrange("(g p t) -> p g t", g=2, t=4))
+        load_rows(g_sb[0], grad_out[0], 2, 4)
+        for j in range(2):
+            load_rows(e_sb[j], edge_w[512 * j : 512 * (j + 1), :], 0, 2)
+            load_rows(e_sb[j], edge_w[512 * j : 512 * (j + 1), :], 2, 4)
+        load_rows(w_sb, weight, 0, 4)
+        load_rows(x_sb[0], x[0], 0, 4)
+        for b in range(1, B):
+            load_rows(g_sb[b], grad_out[b], 0, 4)
+            load_rows(x_sb[b], x[b], 0, 4)
+
+        def new_bank():
+            return psum.tile([P, 512], F32, name="bank", tag="bank")
+
+        def codes(pool, name, bufs=1):
+            c = pool.tile([P, 512], U32, name=name + "_c", align_bytes=64, bufs=bufs)
+            s = pool.tile([P, 512], U8, name=name + "_s", align_bytes=64, bufs=bufs)
+            return c, s
+
+        def quantize(dst, src, fmt):
+            nc.vector.quantize_mx(out=dst[0][:].bitcast(fmt), scales=dst[1][:], in_=src[:].rearrange("p c t -> p (c t)"))
+
+        def flip(src, k, sp):
+            bank = new_bank()
+            for u in range(2):
+                for i in range(2):
+                    words = src[:, 2 * sp + i, :].bitcast(F32)
+                    nc.tensor.transpose(
+                        bank[:, 256 * u + 128 * i : 256 * u + 128 * (i + 1)],
+                        words[:, 256 * k + u : 256 * (k + 1) : 2],
+                        ident[:],
+                    )
+            return bank
+
+        def grouped(tag):
+            return work.tile([P, 512, 4], BF16, name=tag, tag=tag, align_bytes=64, bufs=GROUPED_BUFS[tag])
+
+        def words_out(dst, sp, bank, on_vector=False):
+            out = dst[:, 256 * sp : 256 * (sp + 1), :].rearrange("p r t -> p (r t)").bitcast(F32)
+            out = out.rearrange("p (r u) -> p r u", u=2)
+            in_ = bank[:].rearrange("p (u r) -> p r u", u=2)
+            if on_vector:
+                nc.vector.tensor_copy(out=out, in_=in_)
+            else:
+                nc.scalar.copy(out=out, in_=in_)
+
+        def scaled_out(dst, k, sp, bank):
+            nc.vector.tensor_tensor(
+                out=dst[:, 256 * sp : 256 * (sp + 1), :].rearrange("p r (u e) -> p r u e", u=2),
+                in0=bank[:].bitcast(BF16).rearrange("p (u r e) -> p r u e", u=2, e=2),
+                in1=dv[:, k, :].rearrange("p (u e) -> p u e", u=2).unsqueeze(1).to_broadcast([P, 256, 2, 2]),
+                op=ALU.mult,
+            )
+
+        def mx(bank, sta, cols, sta_fmt, mov, mov_fmt, start, stop):
+            nc.tensor.matmul_mx(
+                out=bank[:],
+                lhsT=sta[0][:, cols].bitcast(sta_fmt),
+                lhsT_scale=sta[1][:, cols],
+                rhs=mov[0][:].bitcast(mov_fmt),
+                rhs_scale=mov[1][:],
+                start=start,
+                stop=stop,
+            )
+
+        def quarter(i):
+            return slice(P * i, P * (i + 1))
+
+        e_q = [[codes(keep, f"e{j}{k}") for k in range(2)] for j in range(2)]
+        w_q = codes(keep, "w")
+        x_q = [codes(keep, f"x{h}") for h in range(HALVES)]
+        za_q = [codes(keep, f"za{h}") for h in range(HALVES)]
+        g_q = {}
+        zb_q = {}
+        d_sb = {}
+        f_sb = {}
+        t_sb = {}
+
+        def x_flip(h):
+            b, k = divmod(h, 2)
+            xt = grouped("xt")
+            for sp in range(2):
+                words_out(xt, sp, flip(x_sb[b], k, sp))
+            return xt
+
+        def g_flip(h):
+            b, k = divmod(h, 2)
+            gt = grouped("gt")
+            for sp in range(2):
+                scaled_out(gt, k, sp, flip(g_sb[b], k, sp))
+            return gt
+
+        def g_quant(h, gt):
+            c = work.tile([P, 512], U32, name="gq_c", tag="gq_c", align_bytes=64, bufs=4)
+            s = work.tile([P, 512], U8, name="gq_s", tag="gq_s", align_bytes=64, bufs=4)
+            g_q[h] = (c, s)
+            quantize(g_q[h], gt, E5M2)
+
+        def first_matmul(h):
+            b, j = divmod(h, 2)
+            d = work.tile([P, 4, 512], BF16, name="d", tag="d", align_bytes=64)
+            d_sb[h] = d
+            for t in range(4):
+                bank = new_bank()
+                for k in range(2):
+                    mx(bank, e_q[j][k], quarter(t), E4M3, g_q[2 * b + k], E5M2, k == 0, k == 1)
+                nc.scalar.activation(
+                    out=d[:, t, :].rearrange("p (u w e) -> p u w e", u=2, e=2),
+                    in_=bank[:].rearrange("p (u e w) -> p u w e", u=2, e=2),
+                    func=ACT.Copy,
+                    scale=dv[:, j, t : t + 1],
+                )
+
+        def d_interleave(h):
+            f = grouped("f")
+            f_sb[h] = f
+            nc.vector.tensor_copy(
+                out=f[:].rearrange("p (c i) t -> p c t i", i=4),
+                in_=d_sb[h][:].rearrange("p t (c i) -> p c t i", i=4),
+            )
+
+        def d_flip(h):
+            zt = grouped("zt")
+            t_sb[h] = zt
+            for sp in range(2):
+                bank = new_bank()
+                for i in range(2):
+                    words = d_sb[h][:, 2 * sp + i, :].bitcast(F32)
+                    for u in range(2):
+                        nc.tensor.transpose(
+                            bank[:, 256 * u + 128 * i : 256 * u + 128 * (i + 1)],
+                            words[:, quarter(u)],
+                            ident[:],
+                        )
+                words_out(zt, sp, bank)
+
+        def zb_quant(h):
+            c = work.tile([P, 512], U32, name="zb_c", tag="zb_c", align_bytes=64)
+            s = work.tile([P, 512], U8, name="zb_s", tag="zb_s", align_bytes=64)
+            zb_q[h] = (c, s)
+            quantize(zb_q[h], t_sb[h], E5M2)
+
+        out_0_view = [out_0[b].rearrange("(p i) s -> p i s", i=4) for b in range(B)]
+
+        def dx_matmul(h):
+            b, j = divmod(h, 2)
+            o = work.tile([P, 4, 512], F32, name="o", tag="o")
+            for i in range(4):
+                bank = new_bank()
+                mx(bank, w_q, quarter(i), E4M3, zb_q[h], E5M2, True, True)
+                out = o[:, i, :].rearrange("p (q t) -> p q t", t=4)
+                in_ = bank[:].rearrange("p (t q) -> p q t", t=4)
+                if i == 3:
+                    nc.vector.tensor_copy(out=out, in_=in_)
+                else:
+                    nc.scalar.copy(out=out, in_=in_)
+                if i % 2 == 1:
+                    nc.sync.dma_start(
+                        out=out_0_view[b][:, i - 1 : i + 1, 512 * j : 512 * (j + 1)], in_=o[:, i - 1 : i + 1, :]
+                    )
+
+        acc = {}
+
+        def dw_matmul(i, passes):
+            for k in passes:
+                if k == 0:
+                    acc[i] = new_bank()
+                mx(acc[i], x_q[k], quarter(i), E4M3, za_q[k], E5M2, k == 0, k == HALVES - 1)
+
+        gts = [grouped("gt"), grouped("gt")]
+        for sp in range(2):
+            for k in range(2):
+                scaled_out(gts[k], k, sp, flip(g_sb[0], k, sp))
+        ets = []
+        for j in range(2):
+            pair = [grouped("f" if j == 0 else "zt") for k in range(2)]
+            ets.append(pair)
+            for sp in range(2):
+                for k in range(2):
+                    words_out(pair[k], sp, flip(e_sb[j], k, sp))
+            if j == 0:
+                for k in range(2):
+                    g_quant(k, gts[k])
+                for k in range(2):
+                    quantize(e_q[0][k], pair[k], E4M3)
+        wt = grouped("zt")
+        for sp in range(2):
+            words_out(wt, sp, flip(w_sb, 0, sp))
+        xts = [x_flip(0), x_flip(1)]
+        for k in range(2):
+            quantize(e_q[1][k], ets[1][k], E4M3)
+        quantize(w_q, wt, E4M3)
+        for k in range(2):
+            quantize(x_q[k], xts[k], E4M3)
+
+        pending_x = None
+        for h in range(HALVES):
+            if h >= 1:
+                d_flip(h - 1)
+                d_interleave(h - 1)
+            gt = None
+            if h + 2 < HALVES:
+                gt = g_flip(h + 2)
+            if h >= 1:
+                quantize(za_q[h - 1], f_sb[h - 1], E5M2)
+            if gt is not None:
+                g_quant(h + 2, gt)
+            if h >= 1:
+                zb_quant(h - 1)
+            first_matmul(h)
+            if h >= 2:
+                dx_matmul(h - 2)
+            if pending_x is not None:
+                quantize(x_q[pending_x[0]], pending_x[1], E4M3)
+                pending_x = None
+            if h + 2 < HALVES:
+                pending_x = (h + 2, x_flip(h + 2))
+            if h == HALVES - 2:
+                dw_matmul(0, range(0, 5))
+            if h == HALVES - 1:
+                dw_matmul(0, range(5, 6))
+                dw_matmul(1, range(0, 6))
+
+        last = HALVES - 1
+        d_flip(last)
+        d_interleave(last)
+        dx_matmul(last - 1)
+        quantize(za_q[last], f_sb[last], E5M2)
+        zb_quant(last)
+        for i in range(2):
+            dw_matmul(i, range(6, last))
+        for i in range(2, 4):
+            dw_matmul(i, range(0, last))
+        dx_matmul(last)
+        r = work.tile([P, 4, 512], F32, name="r", tag="o")
+        out_1_view = out_1.rearrange("(p i) o -> p i o", i=4)
+        for i in range(4):
+            dw_matmul(i, range(last, HALVES))
+            out = r[:, i, :].rearrange("p (w u e) -> p w u e", u=2, e=2)
+            in_ = acc[i][:].rearrange("p (u w e) -> p w u e", u=2, e=2)
+            if i % 2 == 0:
+                nc.vector.tensor_copy(out=out, in_=in_)
+            else:
+                nc.scalar.copy(out=out, in_=in_)
+            nc.sync.dma_start(out=out_1_view[:, i, :], in_=r[:, i, :])

@@ -12,12 +12,15 @@ U32 = mybir.dt.uint32
 U8 = mybir.dt.uint8
 E4M3 = mybir.dt.float8_e4m3fn_x4
 E5M2 = mybir.dt.float8_e5m2_x4
-ACT = mybir.ActivationFunctionType
-ALU = mybir.AluOpType
+COPY = mybir.ActivationFunctionType.Copy
+MULT = mybir.AluOpType.mult
 
 P = 128
 HALVES = 2 * B
-GROUPED_BUFS = {"gt": 3, "zt": 3, "xt": 2, "f": 2}
+LAST = HALVES - 1
+GROUPED_BUFS = {"gt": 3, "zt": 3, "xt": 3, "f": 3}
+SORTED_G = (3, 5)
+SORTED_X = (1, 4, 5, 6, 7)
 
 
 def tile_graphembedding_pa_v_kernel(tc, x, edge_w, weight, bias, dinv, grad_out, out_0, out_1):
@@ -35,26 +38,31 @@ def tile_graphembedding_pa_v_kernel(tc, x, edge_w, weight, bias, dinv, grad_out,
 
         ctx.enter_context(tc.manual_schedule())
 
-        g_sb = [loads.tile([P, 4, N], BF16, name=f"g{b}") for b in range(B)]
-        x_sb = [loads.tile([P, 4, N], BF16, name=f"x{b}") for b in range(B)]
+        g_sb = [loads.tile([P, 4, N], BF16, name=f"g{b}", tag=f"g{b % 3}") for b in range(B)]
+        x_sb = [loads.tile([P, 4, N], BF16, name=f"x{b}", tag=f"x{b % 3}") for b in range(B)]
         e_sb = [loads.tile([P, 4, N], BF16, name=f"e{j}") for j in range(2)]
         w_sb = loads.tile([P, 4, O], BF16, name="w_sb")
 
-        def load_rows(tile, src, lo, hi):
-            view = src.rearrange("(p j) k -> p j k", j=4)
-            nc.sync.dma_start(out=tile[:, lo:hi, :], in_=view[:, lo:hi, :])
+        def load(tile, src, slots=slice(0, 4), cols=slice(None)):
+            view = src.rearrange("(p i) k -> p i k", i=4)
+            nc.sync.dma_start(out=tile[:, slots, cols], in_=view[:, slots, cols])
 
-        load_rows(g_sb[0], grad_out[0], 0, 2)
+        lo, hi = slice(0, 2), slice(2, 4)
+        load(g_sb[0], grad_out[0], lo, slice(0, 512))
         nc.sync.dma_start(out=dv[:], in_=dinv.rearrange("(g p t) -> p g t", g=2, t=4))
-        load_rows(g_sb[0], grad_out[0], 2, 4)
+        load(g_sb[0], grad_out[0], lo, slice(512, 1024))
+        load(g_sb[0], grad_out[0], hi)
         for j in range(2):
-            load_rows(e_sb[j], edge_w[512 * j : 512 * (j + 1), :], 0, 2)
-            load_rows(e_sb[j], edge_w[512 * j : 512 * (j + 1), :], 2, 4)
-        load_rows(w_sb, weight, 0, 4)
-        load_rows(x_sb[0], x[0], 0, 4)
-        for b in range(1, B):
-            load_rows(g_sb[b], grad_out[b], 0, 4)
-            load_rows(x_sb[b], x[b], 0, 4)
+            for slots in (lo, hi):
+                load(e_sb[j], edge_w[512 * j : 512 * (j + 1), :], slots)
+        load(g_sb[1], grad_out[1], cols=slice(0, 512))
+        load(g_sb[1], grad_out[1], cols=slice(512, 1024))
+        load(w_sb, weight)
+        load(x_sb[0], x[0])
+        for b in range(2, B):
+            load(g_sb[b], grad_out[b])
+            load(x_sb[b - 1], x[b - 1])
+        load(x_sb[B - 1], x[B - 1])
 
         def new_bank():
             return psum.tile([P, 512], F32, name="bank", tag="bank")
@@ -67,125 +75,117 @@ def tile_graphembedding_pa_v_kernel(tc, x, edge_w, weight, bias, dinv, grad_out,
         def quantize(dst, src, fmt):
             nc.vector.quantize_mx(out=dst[0][:].bitcast(fmt), scales=dst[1][:], in_=src[:].rearrange("p c t -> p (c t)"))
 
-        def flip(src, k, sp):
+        def part(i):
+            return slice(P * i, P * (i + 1))
+
+        def sort_words(src, k):
+            srt = work.tile([P, 4, 2, P], F32, name="srt", tag="srt")
+            words = src[:, :, 512 * k : 512 * (k + 1)].bitcast(F32)
+            nc.vector.tensor_copy(out=srt[:], in_=words.rearrange("p s (w u) -> p s u w", u=2))
+            return srt
+
+        def flip(src, k, pr, srt=None):
             bank = new_bank()
-            for u in range(2):
-                for i in range(2):
-                    words = src[:, 2 * sp + i, :].bitcast(F32)
-                    nc.tensor.transpose(
-                        bank[:, 256 * u + 128 * i : 256 * u + 128 * (i + 1)],
-                        words[:, 256 * k + u : 256 * (k + 1) : 2],
-                        ident[:],
-                    )
+            for i in range(2):
+                for u in range(2):
+                    if srt is None:
+                        words = src[:, 2 * pr + i, :].bitcast(F32)[:, 256 * k + u : 256 * (k + 1) : 2]
+                    else:
+                        words = srt[:, 2 * pr + i, u, :]
+                    nc.tensor.transpose(bank[:, part(2 * u + i)], words, ident[:])
             return bank
 
         def grouped(tag):
             return work.tile([P, 512, 4], BF16, name=tag, tag=tag, align_bytes=64, bufs=GROUPED_BUFS[tag])
 
-        def words_out(dst, sp, bank, on_vector=False):
-            out = dst[:, 256 * sp : 256 * (sp + 1), :].rearrange("p r t -> p (r t)").bitcast(F32)
-            out = out.rearrange("p (r u) -> p r u", u=2)
-            in_ = bank[:].rearrange("p (u r) -> p r u", u=2)
-            if on_vector:
-                nc.vector.tensor_copy(out=out, in_=in_)
-            else:
-                nc.scalar.copy(out=out, in_=in_)
+        def words_out(dst, pr, bank):
+            out = dst[:, 256 * pr : 256 * (pr + 1), :].rearrange("p r t -> p (r t)").bitcast(F32)
+            nc.scalar.copy(out=out.rearrange("p (r u) -> p r u", u=2), in_=bank[:].rearrange("p (u r) -> p r u", u=2))
 
-        def scaled_out(dst, k, sp, bank):
+        def scaled_out(dst, k, pr, bank):
             nc.vector.tensor_tensor(
-                out=dst[:, 256 * sp : 256 * (sp + 1), :].rearrange("p r (u e) -> p r u e", u=2),
+                out=dst[:, 256 * pr : 256 * (pr + 1), :].rearrange("p r (u e) -> p r u e", u=2),
                 in0=bank[:].bitcast(BF16).rearrange("p (u r e) -> p r u e", u=2, e=2),
                 in1=dv[:, k, :].rearrange("p (u e) -> p u e", u=2).unsqueeze(1).to_broadcast([P, 256, 2, 2]),
-                op=ALU.mult,
+                op=MULT,
             )
 
-        def mx(bank, sta, cols, sta_fmt, mov, mov_fmt, start, stop):
+        def mx(bank, sta, cols, mov, start, stop):
             nc.tensor.matmul_mx(
                 out=bank[:],
-                lhsT=sta[0][:, cols].bitcast(sta_fmt),
+                lhsT=sta[0][:, cols].bitcast(E4M3),
                 lhsT_scale=sta[1][:, cols],
-                rhs=mov[0][:].bitcast(mov_fmt),
+                rhs=mov[0][:].bitcast(E5M2),
                 rhs_scale=mov[1][:],
                 start=start,
                 stop=stop,
             )
 
-        def quarter(i):
-            return slice(P * i, P * (i + 1))
-
         e_q = [[codes(keep, f"e{j}{k}") for k in range(2)] for j in range(2)]
         w_q = codes(keep, "w")
         x_q = [codes(keep, f"x{h}") for h in range(HALVES)]
         za_q = [codes(keep, f"za{h}") for h in range(HALVES)]
-        g_q = {}
-        zb_q = {}
-        d_sb = {}
-        f_sb = {}
-        t_sb = {}
+        g_q, zb_q, d_sb, f_sb, zt_sb, gt_sb, xt_sb, srt_g, srt_x, acc = ({} for i in range(10))
 
         def x_flip(h):
-            b, k = divmod(h, 2)
-            xt = grouped("xt")
-            for sp in range(2):
-                words_out(xt, sp, flip(x_sb[b], k, sp))
-            return xt
+            xt_sb[h] = grouped("xt")
+            for pr in range(2):
+                words_out(xt_sb[h], pr, flip(x_sb[h // 2], h % 2, pr, srt_x.get(h)))
 
         def g_flip(h):
-            b, k = divmod(h, 2)
-            gt = grouped("gt")
-            for sp in range(2):
-                scaled_out(gt, k, sp, flip(g_sb[b], k, sp))
-            return gt
+            gt_sb[h] = grouped("gt")
+            for pr in range(2):
+                scaled_out(gt_sb[h], h % 2, pr, flip(g_sb[h // 2], h % 2, pr, srt_g.get(h)))
 
-        def g_quant(h, gt):
+        def g_quant(h):
             c = work.tile([P, 512], U32, name="gq_c", tag="gq_c", align_bytes=64, bufs=4)
             s = work.tile([P, 512], U8, name="gq_s", tag="gq_s", align_bytes=64, bufs=4)
             g_q[h] = (c, s)
-            quantize(g_q[h], gt, E5M2)
+            quantize(g_q[h], gt_sb[h], E5M2)
+
+        def e_flip(j):
+            pair = [grouped("f" if j else "zt") for k in range(2)]
+            for pr in range(2):
+                for k in range(2):
+                    words_out(pair[k], pr, flip(e_sb[j], k, pr))
+            return pair
 
         def first_matmul(h):
             b, j = divmod(h, 2)
-            d = work.tile([P, 4, 512], BF16, name="d", tag="d", align_bytes=64)
-            d_sb[h] = d
+            d_sb[h] = work.tile([P, 4, 512], BF16, name="d", tag="d", align_bytes=64)
             for t in range(4):
                 bank = new_bank()
                 for k in range(2):
-                    mx(bank, e_q[j][k], quarter(t), E4M3, g_q[2 * b + k], E5M2, k == 0, k == 1)
-                nc.scalar.activation(
-                    out=d[:, t, :].rearrange("p (u w e) -> p u w e", u=2, e=2),
-                    in_=bank[:].rearrange("p (u e w) -> p u w e", u=2, e=2),
-                    func=ACT.Copy,
-                    scale=dv[:, j, t : t + 1],
-                )
+                    mx(bank, e_q[j][k], part(t), g_q[2 * b + k], k == 0, k == 1)
+                out = d_sb[h][:, t, :].rearrange("p (u w e) -> p u w e", u=2, e=2)
+                in_ = bank[:].rearrange("p (u e w) -> p u w e", u=2, e=2)
+                if h >= 5 and t == 3:
+                    nc.vector.tensor_scalar(out=out, in0=in_, scalar1=dv[:, j, t : t + 1], scalar2=None, op0=MULT)
+                else:
+                    nc.scalar.activation(out=out, in_=in_, func=COPY, scale=dv[:, j, t : t + 1])
 
         def d_interleave(h):
-            f = grouped("f")
-            f_sb[h] = f
+            f_sb[h] = grouped("f")
             nc.vector.tensor_copy(
-                out=f[:].rearrange("p (c i) t -> p c t i", i=4),
+                out=f_sb[h][:].rearrange("p (c i) t -> p c t i", i=4),
                 in_=d_sb[h][:].rearrange("p t (c i) -> p c t i", i=4),
             )
 
         def d_flip(h):
-            zt = grouped("zt")
-            t_sb[h] = zt
-            for sp in range(2):
+            zt_sb[h] = grouped("zt")
+            for pr in range(2):
                 bank = new_bank()
                 for i in range(2):
-                    words = d_sb[h][:, 2 * sp + i, :].bitcast(F32)
+                    words = d_sb[h][:, 2 * pr + i, :].bitcast(F32)
                     for u in range(2):
-                        nc.tensor.transpose(
-                            bank[:, 256 * u + 128 * i : 256 * u + 128 * (i + 1)],
-                            words[:, quarter(u)],
-                            ident[:],
-                        )
-                words_out(zt, sp, bank)
+                        nc.tensor.transpose(bank[:, part(2 * u + i)], words[:, part(u)], ident[:])
+                words_out(zt_sb[h], pr, bank)
 
         def zb_quant(h):
             c = work.tile([P, 512], U32, name="zb_c", tag="zb_c", align_bytes=64)
             s = work.tile([P, 512], U8, name="zb_s", tag="zb_s", align_bytes=64)
             zb_q[h] = (c, s)
-            quantize(zb_q[h], t_sb[h], E5M2)
+            quantize(zb_q[h], zt_sb[h], E5M2)
 
         out_0_view = [out_0[b].rearrange("(p i) s -> p i s", i=4) for b in range(B)]
 
@@ -194,10 +194,10 @@ def tile_graphembedding_pa_v_kernel(tc, x, edge_w, weight, bias, dinv, grad_out,
             o = work.tile([P, 4, 512], F32, name="o", tag="o")
             for i in range(4):
                 bank = new_bank()
-                mx(bank, w_q, quarter(i), E4M3, zb_q[h], E5M2, True, True)
+                mx(bank, w_q, part(i), zb_q[h], True, True)
                 out = o[:, i, :].rearrange("p (q t) -> p q t", t=4)
                 in_ = bank[:].rearrange("p (t q) -> p q t", t=4)
-                if i == 3:
+                if h >= 3 and i == 3:
                     nc.vector.tensor_copy(out=out, in_=in_)
                 else:
                     nc.scalar.copy(out=out, in_=in_)
@@ -206,83 +206,15 @@ def tile_graphembedding_pa_v_kernel(tc, x, edge_w, weight, bias, dinv, grad_out,
                         out=out_0_view[b][:, i - 1 : i + 1, 512 * j : 512 * (j + 1)], in_=o[:, i - 1 : i + 1, :]
                     )
 
-        acc = {}
+        out_1_view = out_1.rearrange("(p i) o -> p i o", i=4)
 
         def dw_matmul(i, passes):
             for k in passes:
                 if k == 0:
                     acc[i] = new_bank()
-                mx(acc[i], x_q[k], quarter(i), E4M3, za_q[k], E5M2, k == 0, k == HALVES - 1)
+                mx(acc[i], x_q[k], part(i), za_q[k], k == 0, k == LAST)
 
-        gts = [grouped("gt"), grouped("gt")]
-        for sp in range(2):
-            for k in range(2):
-                scaled_out(gts[k], k, sp, flip(g_sb[0], k, sp))
-        ets = []
-        for j in range(2):
-            pair = [grouped("f" if j == 0 else "zt") for k in range(2)]
-            ets.append(pair)
-            for sp in range(2):
-                for k in range(2):
-                    words_out(pair[k], sp, flip(e_sb[j], k, sp))
-            if j == 0:
-                for k in range(2):
-                    g_quant(k, gts[k])
-                for k in range(2):
-                    quantize(e_q[0][k], pair[k], E4M3)
-        wt = grouped("zt")
-        for sp in range(2):
-            words_out(wt, sp, flip(w_sb, 0, sp))
-        xts = [x_flip(0), x_flip(1)]
-        for k in range(2):
-            quantize(e_q[1][k], ets[1][k], E4M3)
-        quantize(w_q, wt, E4M3)
-        for k in range(2):
-            quantize(x_q[k], xts[k], E4M3)
-
-        pending_x = None
-        for h in range(HALVES):
-            if h >= 1:
-                d_flip(h - 1)
-                d_interleave(h - 1)
-            gt = None
-            if h + 2 < HALVES:
-                gt = g_flip(h + 2)
-            if h >= 1:
-                quantize(za_q[h - 1], f_sb[h - 1], E5M2)
-            if gt is not None:
-                g_quant(h + 2, gt)
-            if h >= 1:
-                zb_quant(h - 1)
-            first_matmul(h)
-            if h >= 2:
-                dx_matmul(h - 2)
-            if pending_x is not None:
-                quantize(x_q[pending_x[0]], pending_x[1], E4M3)
-                pending_x = None
-            if h + 2 < HALVES:
-                pending_x = (h + 2, x_flip(h + 2))
-            if h == HALVES - 2:
-                dw_matmul(0, range(0, 5))
-            if h == HALVES - 1:
-                dw_matmul(0, range(5, 6))
-                dw_matmul(1, range(0, 6))
-
-        last = HALVES - 1
-        d_flip(last)
-        d_interleave(last)
-        dx_matmul(last - 1)
-        quantize(za_q[last], f_sb[last], E5M2)
-        zb_quant(last)
-        for i in range(2):
-            dw_matmul(i, range(6, last))
-        for i in range(2, 4):
-            dw_matmul(i, range(0, last))
-        dx_matmul(last)
-        r = work.tile([P, 4, 512], F32, name="r", tag="o")
-        out_1_view = out_1.rearrange("(p i) o -> p i o", i=4)
-        for i in range(4):
-            dw_matmul(i, range(last, HALVES))
+        def dw_store(i):
             out = r[:, i, :].rearrange("p (w u e) -> p w u e", u=2, e=2)
             in_ = acc[i][:].rearrange("p (u w e) -> p w u e", u=2, e=2)
             if i % 2 == 0:
@@ -290,3 +222,68 @@ def tile_graphembedding_pa_v_kernel(tc, x, edge_w, weight, bias, dinv, grad_out,
             else:
                 nc.scalar.copy(out=out, in_=in_)
             nc.sync.dma_start(out=out_1_view[:, i, :], in_=r[:, i, :])
+
+        gt_sb[0], gt_sb[1] = grouped("gt"), grouped("gt")
+        for pr in range(2):
+            for k in range(2):
+                scaled_out(gt_sb[k], k, pr, flip(g_sb[0], k, pr))
+        for j in range(2):
+            pair = e_flip(j)
+            for k in range(2):
+                if j == 0:
+                    g_quant(k)
+                quantize(e_q[j][k], pair[k], E4M3)
+
+        for h in range(HALVES):
+            if h >= 1:
+                d_flip(h - 1)
+                x_flip(h - 1)
+                d_interleave(h - 1)
+            if h + 2 < HALVES:
+                g_flip(h + 2)
+            first_matmul(h)
+            if h >= 2:
+                quantize(x_q[h - 2], xt_sb[h - 2], E4M3)
+            if h + 2 < HALVES:
+                g_quant(h + 2)
+            if h + 3 in SORTED_G:
+                srt_g[h + 3] = sort_words(g_sb[(h + 3) // 2], (h + 3) % 2)
+            if h == 0:
+                wt = grouped("zt")
+                for pr in range(2):
+                    words_out(wt, pr, flip(w_sb, 0, pr))
+            if h >= 2:
+                dx_matmul(h - 2)
+            if h + 1 in SORTED_X:
+                srt_x[h + 1] = sort_words(x_sb[(h + 1) // 2], (h + 1) % 2)
+            if h >= 1:
+                zb_quant(h - 1)
+            if h >= 2:
+                quantize(za_q[h - 2], f_sb[h - 2], E5M2)
+            if h == 1:
+                quantize(w_q, wt, E4M3)
+            if h == LAST - 1:
+                dw_matmul(0, range(0, 4))
+            if h == LAST:
+                dw_matmul(0, range(4, 5))
+                dw_matmul(1, range(0, 2))
+
+        r = work.tile([P, 4, 512], F32, name="r", tag="o")
+        d_flip(LAST)
+        x_flip(LAST)
+        quantize(za_q[LAST - 1], f_sb[LAST - 1], E5M2)
+        quantize(x_q[LAST - 1], xt_sb[LAST - 1], E4M3)
+        d_interleave(LAST)
+        zb_quant(LAST)
+        quantize(za_q[LAST], f_sb[LAST], E5M2)
+        quantize(x_q[LAST], xt_sb[LAST], E4M3)
+        dx_matmul(LAST - 1)
+        dw_matmul(0, range(5, LAST))
+        dw_matmul(1, range(2, LAST))
+        dx_matmul(LAST)
+        dw_matmul(2, range(0, LAST))
+        for i in range(3):
+            dw_matmul(i, range(LAST, HALVES))
+            dw_store(i)
+        dw_matmul(3, range(0, HALVES))
+        dw_store(3)

@@ -167,8 +167,8 @@ def tile_graphembedding_pa_v_kernel(tc, x, edge_w, weight, bias, dinv, grad_out,
         def d_interleave(h):
             f_sb[h] = grouped("f")
             nc.vector.tensor_copy(
-                out=f_sb[h][:].rearrange("p (c i) t -> p c t i", i=4),
-                in_=d_sb[h][:].rearrange("p t (c i) -> p c t i", i=4),
+                out=f_sb[h][:],
+                in_=d_sb[h][:].rearrange("p t c -> p c t"),
             )
 
         def d_flip(h):

from contextlib import ExitStack

import concourse.mybir as mybir
from concourse.masks import make_identity

B, T, O, N = 4, 512, 512, 1024
FLOPS = 2 * B * O * N * N + 2 * 2 * B * N * O * T

F32 = mybir.dt.float32
BF16 = mybir.dt.bfloat16
U32 = mybir.dt.uint32
U8 = mybir.dt.uint8
E4M3 = mybir.dt.float8_e4m3fn_x4
E5M2 = mybir.dt.float8_e5m2_x4
COPY = mybir.ActivationFunctionType.Copy
MULT = mybir.AluOpType.mult

P = 128
HALVES = 2 * B
LAST = HALVES - 1
GROUPED_BUFS = {"gt": 3, "zt": 3, "xt": 3, "f": 3}
SORTED_G = (3, 5)
SORTED_X = (1, 4, 5, 6, 7)


def tile_graphembedding_pa_v_kernel(tc, x, edge_w, weight, bias, dinv, grad_out, out_0, out_1):
    nc = tc.nc
    with ExitStack() as ctx:
        const = ctx.enter_context(tc.tile_pool(name="const", bufs=1))
        loads = ctx.enter_context(tc.tile_pool(name="loads", bufs=1))
        keep = ctx.enter_context(tc.tile_pool(name="keep", bufs=1))
        work = ctx.enter_context(tc.tile_pool(name="work", bufs=3))
        psum = ctx.enter_context(tc.psum_pool(name="psum", bufs=8))

        ident = const.tile([P, P], F32, name="ident")
        make_identity(nc, ident[:])
        dv = const.tile([P, 2, 4], F32, name="dv")

        ctx.enter_context(tc.manual_schedule())

        g_sb = [loads.tile([P, 4, N], BF16, name=f"g{b}", tag=f"g{b % 3}") for b in range(B)]
        x_sb = [loads.tile([P, 4, N], BF16, name=f"x{b}", tag=f"x{b % 3}") for b in range(B)]
        e_sb = [loads.tile([P, 4, N], BF16, name=f"e{j}") for j in range(2)]
        w_sb = loads.tile([P, 4, O], BF16, name="w_sb")

        def load(tile, src, slots=slice(0, 4), cols=slice(None)):
            view = src.rearrange("(p i) k -> p i k", i=4)
            nc.sync.dma_start(out=tile[:, slots, cols], in_=view[:, slots, cols])

        lo, hi = slice(0, 2), slice(2, 4)
        load(g_sb[0], grad_out[0], lo, slice(0, 512))
        nc.sync.dma_start(out=dv[:], in_=dinv.rearrange("(g p t) -> p g t", g=2, t=4))
        load(g_sb[0], grad_out[0], lo, slice(512, 1024))
        load(g_sb[0], grad_out[0], hi)
        for j in range(2):
            for slots in (lo, hi):
                load(e_sb[j], edge_w[512 * j : 512 * (j + 1), :], slots)
        load(g_sb[1], grad_out[1], cols=slice(0, 512))
        load(g_sb[1], grad_out[1], cols=slice(512, 1024))
        load(w_sb, weight)
        load(x_sb[0], x[0])
        for b in range(2, B):
            load(g_sb[b], grad_out[b])
            load(x_sb[b - 1], x[b - 1])
        load(x_sb[B - 1], x[B - 1])

        def new_bank():
            return psum.tile([P, 512], F32, name="bank", tag="bank")

        def codes(pool, name, bufs=1):
            c = pool.tile([P, 512], U32, name=name + "_c", align_bytes=64, bufs=bufs)
            s = pool.tile([P, 512], U8, name=name + "_s", align_bytes=64, bufs=bufs)
            return c, s

        def quantize(dst, src, fmt):
            nc.vector.quantize_mx(out=dst[0][:].bitcast(fmt), scales=dst[1][:], in_=src[:].rearrange("p c t -> p (c t)"))

        def part(i):
            return slice(P * i, P * (i + 1))

        def sort_words(src, k):
            srt = work.tile([P, 4, 2, P], F32, name="srt", tag="srt")
            words = src[:, :, 512 * k : 512 * (k + 1)].bitcast(F32)
            nc.vector.tensor_copy(out=srt[:], in_=words.rearrange("p s (w u) -> p s u w", u=2))
            return srt

        def flip(src, k, pr, srt=None):
            bank = new_bank()
            for i in range(2):
                for u in range(2):
                    if srt is None:
                        words = src[:, 2 * pr + i, :].bitcast(F32)[:, 256 * k + u : 256 * (k + 1) : 2]
                    else:
                        words = srt[:, 2 * pr + i, u, :]
                    nc.tensor.transpose(bank[:, part(2 * u + i)], words, ident[:])
            return bank

        def grouped(tag):
            return work.tile([P, 512, 4], BF16, name=tag, tag=tag, align_bytes=64, bufs=GROUPED_BUFS[tag])

        def words_out(dst, pr, bank):
            out = dst[:, 256 * pr : 256 * (pr + 1), :].rearrange("p r t -> p (r t)").bitcast(F32)
            nc.scalar.copy(out=out.rearrange("p (r u) -> p r u", u=2), in_=bank[:].rearrange("p (u r) -> p r u", u=2))

        def scaled_out(dst, k, pr, bank):
            nc.vector.tensor_tensor(
                out=dst[:, 256 * pr : 256 * (pr + 1), :].rearrange("p r (u e) -> p r u e", u=2),
                in0=bank[:].bitcast(BF16).rearrange("p (u r e) -> p r u e", u=2, e=2),
                in1=dv[:, k, :].rearrange("p (u e) -> p u e", u=2).unsqueeze(1).to_broadcast([P, 256, 2, 2]),
                op=MULT,
            )

        def mx(bank, sta, cols, mov, start, stop):
            nc.tensor.matmul_mx(
                out=bank[:],
                lhsT=sta[0][:, cols].bitcast(E4M3),
                lhsT_scale=sta[1][:, cols],
                rhs=mov[0][:].bitcast(E5M2),
                rhs_scale=mov[1][:],
                start=start,
                stop=stop,
            )

        e_q = [[codes(keep, f"e{j}{k}") for k in range(2)] for j in range(2)]
        w_q = codes(keep, "w")
        x_q = [codes(keep, f"x{h}") for h in range(HALVES)]
        za_q = [codes(keep, f"za{h}") for h in range(HALVES)]
        g_q, zb_q, d_sb, f_sb, zt_sb, gt_sb, xt_sb, srt_g, srt_x, acc = ({} for i in range(10))

        def x_flip(h):
            xt_sb[h] = grouped("xt")
            for pr in range(2):
                words_out(xt_sb[h], pr, flip(x_sb[h // 2], h % 2, pr, srt_x.get(h)))

        def g_flip(h):
            gt_sb[h] = grouped("gt")
            for pr in range(2):
                scaled_out(gt_sb[h], h % 2, pr, flip(g_sb[h // 2], h % 2, pr, srt_g.get(h)))

        def g_quant(h):
            c = work.tile([P, 512], U32, name="gq_c", tag="gq_c", align_bytes=64, bufs=4)
            s = work.tile([P, 512], U8, name="gq_s", tag="gq_s", align_bytes=64, bufs=4)
            g_q[h] = (c, s)
            quantize(g_q[h], gt_sb[h], E5M2)

        def e_flip(j):
            pair = [grouped("f" if j else "zt") for k in range(2)]
            for pr in range(2):
                for k in range(2):
                    words_out(pair[k], pr, flip(e_sb[j], k, pr))
            return pair

        def first_matmul(h):
            b, j = divmod(h, 2)
            d_sb[h] = work.tile([P, 4, 512], BF16, name="d", tag="d", align_bytes=64)
            for t in range(4):
                bank = new_bank()
                for k in range(2):
                    mx(bank, e_q[j][k], part(t), g_q[2 * b + k], k == 0, k == 1)
                out = d_sb[h][:, t, :].rearrange("p (u w e) -> p u w e", u=2, e=2)
                in_ = bank[:].rearrange("p (u e w) -> p u w e", u=2, e=2)
                if h >= 5 and t == 3:
                    nc.vector.tensor_scalar(out=out, in0=in_, scalar1=dv[:, j, t : t + 1], scalar2=None, op0=MULT)
                else:
                    nc.scalar.activation(out=out, in_=in_, func=COPY, scale=dv[:, j, t : t + 1])

        def d_interleave(h):
            f_sb[h] = grouped("f")
            nc.vector.tensor_copy(
                out=f_sb[h][:],
                in_=d_sb[h][:].rearrange("p t c -> p c t"),
            )

        def d_flip(h):
            zt_sb[h] = grouped("zt")
            for pr in range(2):
                bank = new_bank()
                for i in range(2):
                    words = d_sb[h][:, 2 * pr + i, :].bitcast(F32)
                    for u in range(2):
                        nc.tensor.transpose(bank[:, part(2 * u + i)], words[:, part(u)], ident[:])
                words_out(zt_sb[h], pr, bank)

        def zb_quant(h):
            c = work.tile([P, 512], U32, name="zb_c", tag="zb_c", align_bytes=64)
            s = work.tile([P, 512], U8, name="zb_s", tag="zb_s", align_bytes=64)
            zb_q[h] = (c, s)
            quantize(zb_q[h], zt_sb[h], E5M2)

        out_0_view = [out_0[b].rearrange("(p i) s -> p i s", i=4) for b in range(B)]

        def dx_matmul(h):
            b, j = divmod(h, 2)
            o = work.tile([P, 4, 512], F32, name="o", tag="o")
            for i in range(4):
                bank = new_bank()
                mx(bank, w_q, part(i), zb_q[h], True, True)
                out = o[:, i, :].rearrange("p (q t) -> p q t", t=4)
                in_ = bank[:].rearrange("p (t q) -> p q t", t=4)
                if h >= 3 and i == 3:
                    nc.vector.tensor_copy(out=out, in_=in_)
                else:
                    nc.scalar.copy(out=out, in_=in_)
                if i % 2 == 1:
                    nc.sync.dma_start(
                        out=out_0_view[b][:, i - 1 : i + 1, 512 * j : 512 * (j + 1)], in_=o[:, i - 1 : i + 1, :]
                    )

        out_1_view = out_1.rearrange("(p i) o -> p i o", i=4)

        def dw_matmul(i, passes):
            for k in passes:
                if k == 0:
                    acc[i] = new_bank()
                mx(acc[i], x_q[k], part(i), za_q[k], k == 0, k == LAST)

        def dw_store(i):
            out = r[:, i, :].rearrange("p (w u e) -> p w u e", u=2, e=2)
            in_ = acc[i][:].rearrange("p (u w e) -> p w u e", u=2, e=2)
            if i % 2 == 0:
                nc.vector.tensor_copy(out=out, in_=in_)
            else:
                nc.scalar.copy(out=out, in_=in_)
            nc.sync.dma_start(out=out_1_view[:, i, :], in_=r[:, i, :])

        gt_sb[0], gt_sb[1] = grouped("gt"), grouped("gt")
        for pr in range(2):
            for k in range(2):
                scaled_out(gt_sb[k], k, pr, flip(g_sb[0], k, pr))
        for j in range(2):
            pair = e_flip(j)
            for k in range(2):
                if j == 0:
                    g_quant(k)
                quantize(e_q[j][k], pair[k], E4M3)

        for h in range(HALVES):
            if h >= 1:
                d_flip(h - 1)
                x_flip(h - 1)
                d_interleave(h - 1)
            if h + 2 < HALVES:
                g_flip(h + 2)
            first_matmul(h)
            if h >= 2:
                quantize(x_q[h - 2], xt_sb[h - 2], E4M3)
            if h + 2 < HALVES:
                g_quant(h + 2)
            if h + 3 in SORTED_G:
                srt_g[h + 3] = sort_words(g_sb[(h + 3) // 2], (h + 3) % 2)
            if h == 0:
                wt = grouped("zt")
                for pr in range(2):
                    words_out(wt, pr, flip(w_sb, 0, pr))
            if h >= 2:
                dx_matmul(h - 2)
            if h + 1 in SORTED_X:
                srt_x[h + 1] = sort_words(x_sb[(h + 1) // 2], (h + 1) % 2)
            if h >= 1:
                zb_quant(h - 1)
            if h >= 2:
                quantize(za_q[h - 2], f_sb[h - 2], E5M2)
            if h == 1:
                quantize(w_q, wt, E4M3)
            if h == LAST - 1:
                dw_matmul(0, range(0, 4))
            if h == LAST:
                dw_matmul(0, range(4, 5))
                dw_matmul(1, range(0, 2))

        r = work.tile([P, 4, 512], F32, name="r", tag="o")
        d_flip(LAST)
        x_flip(LAST)
        quantize(za_q[LAST - 1], f_sb[LAST - 1], E5M2)
        quantize(x_q[LAST - 1], xt_sb[LAST - 1], E4M3)
        d_interleave(LAST)
        zb_quant(LAST)
        quantize(za_q[LAST], f_sb[LAST], E5M2)
        quantize(x_q[LAST], xt_sb[LAST], E4M3)
        dx_matmul(LAST - 1)
        dw_matmul(0, range(5, LAST))
        dw_matmul(1, range(2, LAST))
        dx_matmul(LAST)
        dw_matmul(2, range(0, LAST))
        for i in range(3):
            dw_matmul(i, range(LAST, HALVES))
            dw_store(i)
        dw_matmul(3, range(0, HALVES))
        dw_store(3)
